import numpy as np
import ml_dtypes


def mxq(x, axis, fmt="e4m3"):
    dtype, down = {"e4m3": (ml_dtypes.float8_e4m3fn, 7), "e5m2": (ml_dtypes.float8_e5m2, 14)}[fmt]
    v = np.moveaxis(np.asarray(x, np.float32).astype(ml_dtypes.bfloat16).astype(np.float64), axis, -1)
    blocks = v.reshape(v.shape[:-1] + (-1, 32))
    amax = np.abs(blocks).max(-1, keepdims=True)
    byte = np.maximum(np.where(amax > 0, np.frexp(amax)[1] - 1 + 127, 0) - down, 1)
    scale = np.exp2(byte - 127.0)
    codes = (blocks / scale).astype(np.float32).astype(dtype).astype(np.float64)
    return np.moveaxis((codes * scale).reshape(v.shape), -1, axis)


WIDE = False


def mx_kscale(k):
    if not WIDE:
        return np.ones(k)
    levels = np.array([20, -20, 10, -10, 0])
    a = np.random.permutation(np.resize(levels, k // 512 * 4)).reshape(k // 512, 4)
    idx = np.arange(k)
    return np.exp2(a[idx // 512, idx % 128 // 32])


BF16 = ml_dtypes.bfloat16


def bf(x):
    return np.asarray(x, np.float32).astype(BF16)


def f64(x):
    return np.asarray(x).astype(np.float64)


B, NH, T, D, N = 1, 1, 128, 512, 1024
THETA = 2.0 ** 16
SCALE = N ** -0.5


def rope_tables():
    pair = np.repeat(np.arange(N // 2), 2)
    freqs = 1.0 / THETA ** (pair * 2.0 / N)
    angles = np.arange(T)[:, None] * freqs[None, :]
    return np.cos(angles), np.sin(angles)


def rope(v, cos, sin):
    v_rot = np.stack([-v[..., 1::2], v[..., ::2]], axis=-1).reshape(v.shape)
    return v * cos + v_rot * sin


def rope_adjoint(h, cos, sin):
    hs = h * sin
    hs_rot = np.stack([hs[..., 1::2], -hs[..., ::2]], axis=-1).reshape(h.shape)
    return h * cos + hs_rot


def setup_inputs():
    u = mx_kscale(D)
    cos, sin = rope_tables()
    Q = np.random.uniform(size=(B, NH, T, N)) * 1.2 / N ** 0.25
    V = np.random.standard_normal((B, 1, T, D)) * 45.0 / np.sqrt(T) / u
    state = np.random.standard_normal((B, NH, N, D)) * 60.0 / N ** 0.75 / u
    g = np.random.standard_normal((B, NH, N, D)) * np.exp2(np.random.randint(-12, 1, (B, NH, N, 1))) * 32.0 * u
    return {"Q": bf(Q), "V": bf(V), "state": bf(state), "cos": bf(cos), "sin": bf(sin), "grad_out": bf(g)}


def reference(Q, V, state, cos, sin, grad_out):
    gQR = (mxq(f64(V), 3, "e4m3") @ np.swapaxes(mxq(f64(grad_out), 3, "e5m2"), -2, -1)) * SCALE
    return rope_adjoint(gQR, f64(cos), f64(sin))

@@ -1,0 +1,139 @@
+import concourse.mybir as mybir
+from concourse.masks import make_identity
+
+F32 = mybir.dt.float32
+BF16 = mybir.dt.bfloat16
+U32 = mybir.dt.uint32
+U8 = mybir.dt.uint8
+E4M3_X4 = mybir.dt.float8_e4m3fn_x4
+E5M2_X4 = mybir.dt.float8_e5m2_x4
+MULT = mybir.AluOpType.mult
+ADD = mybir.AluOpType.add
+
+P = 128
+PACK = 4
+T = 128
+D = 512
+N = 1024
+SCALE = N ** -0.5
+
+HALVES = D // 2 // P
+BANK = 512
+N_BANKS = N // BANK
+PLANES = BANK // P
+CHUNK = 2
+
+FLOPS = 2 * T * N * D
+BYTES = 2 * (T * D + N * D + 2 * T * N) + 4 * T * N
+
+
+def transpose_row_tile(nc, psum, rows, ident):
+    words = rows.bitcast(F32)
+    turned = psum.tile([P, HALVES, P], F32, tag="turned")
+    for u in range(HALVES):
+        nc.tensor.transpose(turned[:, u, :], words[:, u * P : (u + 1) * P], ident)
+    return turned
+
+
+def group_words(copy, grouped, turned):
+    copy(out=grouped.bitcast(F32), in_=turned[:].rearrange("p u r -> p r u"))
+
+
+def tile_attention_pb_s_kernel(tc, Q, V, state, cos, sin, grad_out, out):
+    nc = tc.nc
+    v_rows_dram = V.flatten_outer_dims()
+    out_dram = out.flatten_outer_dims()
+    g_dram = grad_out.flatten_outer_dims().rearrange("(b p j) d -> b p j d", b=N_BANKS, p=P, j=PLANES)
+
+    with (
+        tc.tile_pool(name="keep", bufs=1) as keep,
+        tc.tile_pool(name="loads", bufs=N_BANKS * PLANES // CHUNK) as loads,
+        tc.tile_pool(name="banks", bufs=N_BANKS) as banks,
+        tc.psum_pool(name="psum_turn", bufs=6) as psum_turn,
+        tc.psum_pool(name="psum_h", bufs=N_BANKS) as psum_h,
+    ):
+        ident = keep.tile([P, P], F32)
+        make_identity(nc, ident[:])
+
+        v_rows = keep.tile([T, D], BF16)
+        nc.sync.dma_start(out=v_rows[:], in_=v_rows_dram)
+        g_chunks = []
+        for b in range(N_BANKS):
+            for j in range(0, PLANES, CHUNK):
+                g_rows = loads.tile([P, CHUNK, D], BF16)
+                nc.sync.dma_start(out=g_rows[:], in_=g_dram[b, :, j : j + CHUNK, :])
+                g_chunks.append(g_rows)
+        cos_sb = keep.tile([T, N], BF16)
+        nc.sync.dma_start(out=cos_sb[:], in_=cos)
+        sin_sb = keep.tile([T, N], BF16)
+        nc.sync.dma_start(out=sin_sb[:], in_=sin)
+
+        v_grouped = keep.tile([P, T, PACK], BF16, align_bytes=64)
+        v_codes = keep.tile([P, T], U32, align_bytes=64)
+        v_scales = keep.tile([P, T], U8, align_bytes=64)
+        v_turned = transpose_row_tile(nc, psum_turn, v_rows[:], ident[:])
+        group_words(nc.vector.tensor_copy, v_grouped[:], v_turned)
+        nc.vector.quantize_mx(
+            out=v_codes[:].bitcast(E4M3_X4),
+            scales=v_scales[:],
+            in_=v_grouped[:].rearrange("p r t -> p (r t)"),
+        )
+
+        for b in range(N_BANKS):
+            g_grouped = banks.tile([P, PLANES, P, PACK], BF16, align_bytes=64)
+            g_codes = banks.tile([P, PLANES, P], U32, align_bytes=64)
+            g_scales = banks.tile([P, PLANES, P], U8, align_bytes=64)
+            for j in range(0, PLANES, CHUNK):
+                g_rows = g_chunks[(b * PLANES + j) // CHUNK]
+                for a in range(CHUNK):
+                    g_turned = transpose_row_tile(nc, psum_turn, g_rows[:, a, :], ident[:])
+                    copy = nc.scalar.copy if a % 2 == 0 else nc.vector.tensor_copy
+                    group_words(copy, g_grouped[:, j + a, :, :], g_turned)
+                nc.vector.quantize_mx(
+                    out=g_codes[:, j : j + CHUNK, :].rearrange("p j r -> p (j r)").bitcast(E5M2_X4),
+                    scales=g_scales[:, j : j + CHUNK, :].rearrange("p j r -> p (j r)"),
+                    in_=g_grouped[:, j : j + CHUNK, :, :].rearrange("p j r t -> p (j r t)"),
+                )
+
+            h = psum_h.tile([T, BANK], F32)
+            nc.tensor.matmul_mx(
+                out=h[:],
+                lhsT=v_codes[:].bitcast(E4M3_X4),
+                lhsT_scale=v_scales[:],
+                rhs=g_codes[:].rearrange("p j r -> p (j r)").bitcast(E5M2_X4),
+                rhs_scale=g_scales[:].rearrange("p j r -> p (j r)"),
+                start=True,
+                stop=True,
+            )
+
+            cols = slice(b * BANK, (b + 1) * BANK)
+            direct = banks.tile([T, BANK], F32)
+            nc.vector.scalar_tensor_tensor(
+                out=direct[:].rearrange("t (p j) -> t p j", j=PLANES),
+                in0=h[:].rearrange("t (j p) -> t p j", j=PLANES),
+                scalar=SCALE,
+                in1=cos_sb[:, cols].rearrange("t (p j) -> t p j", j=PLANES),
+                op0=MULT,
+                op1=MULT,
+            )
+            crossed = banks.tile([T, 2, BANK // 2], F32)
+            h_by_parity = h[:].rearrange("t (m e p) -> t e p m", m=PLANES // 2, e=2)
+            sin_by_parity = sin_sb[:, cols].rearrange("t (p m e) -> t e p m", m=PLANES // 2, e=2)
+            for e in range(2):
+                partner = 1 - e
+                nc.vector.scalar_tensor_tensor(
+                    out=crossed[:, e, :].rearrange("t (p m) -> t p m", m=PLANES // 2),
+                    in0=h_by_parity[:, partner],
+                    scalar=SCALE if e == 0 else -SCALE,
+                    in1=sin_by_parity[:, partner],
+                    op0=MULT,
+                    op1=MULT,
+                )
+            result = banks.tile([T, BANK], F32)
+            nc.vector.tensor_tensor(
+                out=result[:].rearrange("t (i e) -> t i e", e=2),
+                in0=direct[:].rearrange("t (i e) -> t i e", e=2),
+                in1=crossed[:].rearrange("t e i -> t i e"),
+                op=ADD,
+            )
+            nc.sync.dma_start(out=out_dram[:, cols], in_=result[:])

@@ -48,9 +48,11 @@ def tile_attention_pb_s_kernel(tc, Q, V, state, cos, sin, grad_out, out):
     with (
         tc.tile_pool(name="keep", bufs=1) as keep,
         tc.tile_pool(name="loads", bufs=N_BANKS * PLANES // CHUNK) as loads,
+        tc.tile_pool(name="planes", bufs=N_BANKS * PLANES) as planes,
         tc.tile_pool(name="banks", bufs=N_BANKS) as banks,
         tc.psum_pool(name="psum_turn", bufs=6) as psum_turn,
         tc.psum_pool(name="psum_h", bufs=N_BANKS) as psum_h,
+        tc.manual_schedule(),
     ):
         ident = keep.tile([P, P], F32)
         make_identity(nc, ident[:])
@@ -63,10 +65,16 @@ def tile_attention_pb_s_kernel(tc, Q, V, state, cos, sin, grad_out, out):
                 g_rows = loads.tile([P, CHUNK, D], BF16)
                 nc.sync.dma_start(out=g_rows[:], in_=g_dram[b, :, j : j + CHUNK, :])
                 g_chunks.append(g_rows)
-        cos_sb = keep.tile([T, N], BF16)
-        nc.sync.dma_start(out=cos_sb[:], in_=cos)
-        sin_sb = keep.tile([T, N], BF16)
-        nc.sync.dma_start(out=sin_sb[:], in_=sin)
+        cos_banks = []
+        sin_banks = []
+        for b in range(N_BANKS):
+            cols = slice(b * BANK, (b + 1) * BANK)
+            cos_sb = banks.tile([T, BANK], BF16)
+            nc.sync.dma_start(out=cos_sb[:], in_=cos[:, cols])
+            cos_banks.append(cos_sb)
+            sin_sb = banks.tile([T, BANK], BF16)
+            nc.sync.dma_start(out=sin_sb[:], in_=sin[:, cols])
+            sin_banks.append(sin_sb)
 
         v_grouped = keep.tile([P, T, PACK], BF16, align_bytes=64)
         v_codes = keep.tile([P, T], U32, align_bytes=64)
@@ -79,46 +87,48 @@ def tile_attention_pb_s_kernel(tc, Q, V, state, cos, sin, grad_out, out):
             in_=v_grouped[:].rearrange("p r t -> p (r t)"),
         )
 
+        code_banks = []
+        scale_banks = []
         for b in range(N_BANKS):
-            g_grouped = banks.tile([P, PLANES, P, PACK], BF16, align_bytes=64)
             g_codes = banks.tile([P, PLANES, P], U32, align_bytes=64)
             g_scales = banks.tile([P, PLANES, P], U8, align_bytes=64)
-            for j in range(0, PLANES, CHUNK):
+            for j in range(PLANES):
                 g_rows = g_chunks[(b * PLANES + j) // CHUNK]
-                for a in range(CHUNK):
-                    g_turned = transpose_row_tile(nc, psum_turn, g_rows[:, a, :], ident[:])
-                    copy = nc.scalar.copy if a % 2 == 0 else nc.vector.tensor_copy
-                    group_words(copy, g_grouped[:, j + a, :, :], g_turned)
+                g_turned = transpose_row_tile(nc, psum_turn, g_rows[:, j % CHUNK, :], ident[:])
+                g_grouped = planes.tile([P, P, PACK], BF16, align_bytes=64)
+                group_words(nc.scalar.copy, g_grouped[:], g_turned)
                 nc.vector.quantize_mx(
-                    out=g_codes[:, j : j + CHUNK, :].rearrange("p j r -> p (j r)").bitcast(E5M2_X4),
-                    scales=g_scales[:, j : j + CHUNK, :].rearrange("p j r -> p (j r)"),
-                    in_=g_grouped[:, j : j + CHUNK, :, :].rearrange("p j r t -> p (j r t)"),
+                    out=g_codes[:, j, :].bitcast(E5M2_X4),
+                    scales=g_scales[:, j, :],
+                    in_=g_grouped[:].rearrange("p r t -> p (r t)"),
                 )
+            code_banks.append(g_codes)
+            scale_banks.append(g_scales)
 
+        for b in range(N_BANKS):
             h = psum_h.tile([T, BANK], F32)
             nc.tensor.matmul_mx(
                 out=h[:],
                 lhsT=v_codes[:].bitcast(E4M3_X4),
                 lhsT_scale=v_scales[:],
-                rhs=g_codes[:].rearrange("p j r -> p (j r)").bitcast(E5M2_X4),
-                rhs_scale=g_scales[:].rearrange("p j r -> p (j r)"),
+                rhs=code_banks[b][:].rearrange("p j r -> p (j r)").bitcast(E5M2_X4),
+                rhs_scale=scale_banks[b][:].rearrange("p j r -> p (j r)"),
                 start=True,
                 stop=True,
             )
 
-            cols = slice(b * BANK, (b + 1) * BANK)
             direct = banks.tile([T, BANK], F32)
             nc.vector.scalar_tensor_tensor(
                 out=direct[:].rearrange("t (p j) -> t p j", j=PLANES),
                 in0=h[:].rearrange("t (j p) -> t p j", j=PLANES),
                 scalar=SCALE,
-                in1=cos_sb[:, cols].rearrange("t (p j) -> t p j", j=PLANES),
+                in1=cos_banks[b][:].rearrange("t (p j) -> t p j", j=PLANES),
                 op0=MULT,
                 op1=MULT,
             )
             crossed = banks.tile([T, 2, BANK // 2], F32)
             h_by_parity = h[:].rearrange("t (m e p) -> t e p m", m=PLANES // 2, e=2)
-            sin_by_parity = sin_sb[:, cols].rearrange("t (p m e) -> t e p m", m=PLANES // 2, e=2)
+            sin_by_parity = sin_banks[b][:].rearrange("t (p m e) -> t e p m", m=PLANES // 2, e=2)
             for e in range(2):
                 partner = 1 - e
                 nc.vector.scalar_tensor_tensor(
@@ -136,4 +146,4 @@ def tile_attention_pb_s_kernel(tc, Q, V, state, cos, sin, grad_out, out):
                 in1=crossed[:].rearrange("t e i -> t i e"),
                 op=ADD,
             )
-            nc.sync.dma_start(out=out_dram[:, cols], in_=result[:])
+            nc.sync.dma_start(out=out_dram[:, b * BANK : (b + 1) * BANK], in_=result[:])

@@ -139,8 +139,9 @@ def tile_attention_pb_s_kernel(tc, Q, V, state, cos, sin, grad_out, out):
                     op0=MULT,
                     op1=MULT,
                 )
+            adder = nc.vector if b == N_BANKS - 1 else nc.gpsimd
             result = banks.tile([T, BANK], F32)
-            nc.vector.tensor_tensor(
+            adder.tensor_tensor(
                 out=result[:].rearrange("t (i e) -> t i e", e=2),
                 in0=direct[:].rearrange("t (i e) -> t i e", e=2),
                 in1=crossed[:].rearrange("t e i -> t i e"),

@@ -18,16 +18,18 @@ N = 1024
 SCALE = N ** -0.5
 
 HALVES = D // 2 // P
+PARITIES = 2
+CHUNK = P * PARITIES
 BANK = 512
 N_BANKS = N // BANK
-PLANES = BANK // P
-CHUNK = 2
+CHUNKS = BANK // CHUNK
+TURN_BANKS = 8 - N_BANKS
 
 FLOPS = 2 * T * N * D
 BYTES = 2 * (T * D + N * D + 2 * T * N) + 4 * T * N
 
 
-def transpose_row_tile(nc, psum, rows, ident):
+def transpose_rows(nc, psum, rows, ident):
     words = rows.bitcast(F32)
     turned = psum.tile([P, HALVES, P], F32, tag="turned")
     for u in range(HALVES):
@@ -41,16 +43,16 @@ def group_words(copy, grouped, turned):
 
 def tile_attention_pb_s_kernel(tc, Q, V, state, cos, sin, grad_out, out):
     nc = tc.nc
-    v_rows_dram = V.flatten_outer_dims()
+    v_dram = V.flatten_outer_dims()
     out_dram = out.flatten_outer_dims()
-    g_dram = grad_out.flatten_outer_dims().rearrange("(b p j) d -> b p j d", b=N_BANKS, p=P, j=PLANES)
+    g_dram = grad_out.flatten_outer_dims().rearrange("(c p e) d -> c p e d", p=P, e=PARITIES)
 
     with (
         tc.tile_pool(name="keep", bufs=1) as keep,
-        tc.tile_pool(name="loads", bufs=N_BANKS * PLANES // CHUNK) as loads,
-        tc.tile_pool(name="planes", bufs=N_BANKS * PLANES) as planes,
         tc.tile_pool(name="banks", bufs=N_BANKS) as banks,
-        tc.psum_pool(name="psum_turn", bufs=6) as psum_turn,
+        tc.tile_pool(name="chunks", bufs=N_BANKS * CHUNKS) as chunks,
+        tc.tile_pool(name="planes", bufs=N_BANKS * CHUNKS * PARITIES) as planes,
+        tc.psum_pool(name="psum_turn", bufs=TURN_BANKS) as psum_turn,
         tc.psum_pool(name="psum_h", bufs=N_BANKS) as psum_h,
         tc.manual_schedule(),
     ):
@@ -58,28 +60,27 @@ def tile_attention_pb_s_kernel(tc, Q, V, state, cos, sin, grad_out, out):
         make_identity(nc, ident[:])
 
         v_rows = keep.tile([T, D], BF16)
-        nc.sync.dma_start(out=v_rows[:], in_=v_rows_dram)
+        nc.sync.dma_start(out=v_rows[:], in_=v_dram)
         g_chunks = []
-        for b in range(N_BANKS):
-            for j in range(0, PLANES, CHUNK):
-                g_rows = loads.tile([P, CHUNK, D], BF16)
-                nc.sync.dma_start(out=g_rows[:], in_=g_dram[b, :, j : j + CHUNK, :])
-                g_chunks.append(g_rows)
-        cos_banks = []
+        for c in range(N_BANKS * CHUNKS):
+            g_rows = chunks.tile([P, PARITIES, D], BF16)
+            nc.sync.dma_start(out=g_rows[:], in_=g_dram[c])
+            g_chunks.append(g_rows)
         sin_banks = []
+        cos_banks = []
         for b in range(N_BANKS):
             cols = slice(b * BANK, (b + 1) * BANK)
-            cos_sb = banks.tile([T, BANK], BF16)
-            nc.sync.dma_start(out=cos_sb[:], in_=cos[:, cols])
-            cos_banks.append(cos_sb)
             sin_sb = banks.tile([T, BANK], BF16)
             nc.sync.dma_start(out=sin_sb[:], in_=sin[:, cols])
             sin_banks.append(sin_sb)
+            cos_sb = banks.tile([T, BANK], BF16)
+            nc.sync.dma_start(out=cos_sb[:], in_=cos[:, cols])
+            cos_banks.append(cos_sb)
 
         v_grouped = keep.tile([P, T, PACK], BF16, align_bytes=64)
         v_codes = keep.tile([P, T], U32, align_bytes=64)
         v_scales = keep.tile([P, T], U8, align_bytes=64)
-        v_turned = transpose_row_tile(nc, psum_turn, v_rows[:], ident[:])
+        v_turned = transpose_rows(nc, psum_turn, v_rows[:], ident[:])
         group_words(nc.vector.tensor_copy, v_grouped[:], v_turned)
         nc.vector.quantize_mx(
             out=v_codes[:].bitcast(E4M3_X4),
@@ -90,18 +91,18 @@ def tile_attention_pb_s_kernel(tc, Q, V, state, cos, sin, grad_out, out):
         code_banks = []
         scale_banks = []
         for b in range(N_BANKS):
-            g_codes = banks.tile([P, PLANES, P], U32, align_bytes=64)
-            g_scales = banks.tile([P, PLANES, P], U8, align_bytes=64)
-            for j in range(PLANES):
-                g_rows = g_chunks[(b * PLANES + j) // CHUNK]
-                g_turned = transpose_row_tile(nc, psum_turn, g_rows[:, j % CHUNK, :], ident[:])
-                g_grouped = planes.tile([P, P, PACK], BF16, align_bytes=64)
-                group_words(nc.scalar.copy, g_grouped[:], g_turned)
-                nc.vector.quantize_mx(
-                    out=g_codes[:, j, :].bitcast(E5M2_X4),
-                    scales=g_scales[:, j, :],
-                    in_=g_grouped[:].rearrange("p r t -> p (r t)"),
-                )
+            g_codes = banks.tile([P, CHUNKS, PARITIES, P], U32, align_bytes=64)
+            g_scales = banks.tile([P, CHUNKS, PARITIES, P], U8, align_bytes=64)
+            for c in range(CHUNKS):
+                for e in range(PARITIES):
+                    g_turned = transpose_rows(nc, psum_turn, g_chunks[b * CHUNKS + c][:, e, :], ident[:])
+                    g_grouped = planes.tile([P, P, PACK], BF16, align_bytes=64)
+                    group_words(nc.scalar.copy, g_grouped[:], g_turned)
+                    nc.vector.quantize_mx(
+                        out=g_codes[:, c, e, :].bitcast(E5M2_X4),
+                        scales=g_scales[:, c, e, :],
+                        in_=g_grouped[:].rearrange("p r t -> p (r t)"),
+                    )
             code_banks.append(g_codes)
             scale_banks.append(g_scales)
 
@@ -111,40 +112,49 @@ def tile_attention_pb_s_kernel(tc, Q, V, state, cos, sin, grad_out, out):
                 out=h[:],
                 lhsT=v_codes[:].bitcast(E4M3_X4),
                 lhsT_scale=v_scales[:],
-                rhs=code_banks[b][:].rearrange("p j r -> p (j r)").bitcast(E5M2_X4),
-                rhs_scale=scale_banks[b][:].rearrange("p j r -> p (j r)"),
+                rhs=code_banks[b][:].rearrange("p c e r -> p (c e r)").bitcast(E5M2_X4),
+                rhs_scale=scale_banks[b][:].rearrange("p c e r -> p (c e r)"),
                 start=True,
                 stop=True,
             )
 
-            direct = banks.tile([T, BANK], F32)
-            nc.vector.scalar_tensor_tensor(
-                out=direct[:].rearrange("t (p j) -> t p j", j=PLANES),
-                in0=h[:].rearrange("t (j p) -> t p j", j=PLANES),
-                scalar=SCALE,
-                in1=cos_banks[b][:].rearrange("t (p j) -> t p j", j=PLANES),
-                op0=MULT,
-                op1=MULT,
-            )
-            crossed = banks.tile([T, 2, BANK // 2], F32)
-            h_by_parity = h[:].rearrange("t (m e p) -> t e p m", m=PLANES // 2, e=2)
-            sin_by_parity = sin_banks[b][:].rearrange("t (p m e) -> t e p m", m=PLANES // 2, e=2)
-            for e in range(2):
+            crossed = banks.tile([T, PARITIES, CHUNKS, P], F32)
+            h_by_parity = h[:].rearrange("t (c e p) -> t e c p", c=CHUNKS, e=PARITIES)
+            sin_by_parity = sin_banks[b][:].rearrange("t (c p e) -> t e c p", c=CHUNKS, e=PARITIES)
+            for e in range(PARITIES):
                 partner = 1 - e
                 nc.vector.scalar_tensor_tensor(
-                    out=crossed[:, e, :].rearrange("t (p m) -> t p m", m=PLANES // 2),
+                    out=crossed[:, e, :, :],
                     in0=h_by_parity[:, partner],
                     scalar=SCALE if e == 0 else -SCALE,
                     in1=sin_by_parity[:, partner],
                     op0=MULT,
                     op1=MULT,
                 )
+            directs = []
+            for c in range(CHUNKS):
+                cols = slice(c * CHUNK, (c + 1) * CHUNK)
+                direct = chunks.tile([T, P, PARITIES], F32)
+                nc.vector.scalar_tensor_tensor(
+                    out=direct[:],
+                    in0=h[:, cols].rearrange("t (e p) -> t p e", e=PARITIES),
+                    scalar=SCALE,
+                    in1=cos_banks[b][:, cols].rearrange("t (p e) -> t p e", e=PARITIES),
+                    op0=MULT,
+                    op1=MULT,
+                )
+                directs.append(direct)
             adder = nc.vector if b == N_BANKS - 1 else nc.gpsimd
-            result = banks.tile([T, BANK], F32)
-            adder.tensor_tensor(
-                out=result[:].rearrange("t (i e) -> t i e", e=2),
-                in0=direct[:].rearrange("t (i e) -> t i e", e=2),
-                in1=crossed[:].rearrange("t e i -> t i e"),
-                op=ADD,
-            )
-            nc.sync.dma_start(out=out_dram[:, b * BANK : (b + 1) * BANK], in_=result[:])
+            for c in range(CHUNKS):
+                result = chunks.tile([T, P, PARITIES], F32)
+                adder.tensor_tensor(
+                    out=result[:],
+                    in0=directs[c][:],
+                    in1=crossed[:, :, c, :].rearrange("t e p -> t p e"),
+                    op=ADD,
+                )
+                first = b * BANK + c * CHUNK
+                nc.sync.dma_start(
+                    out=out_dram[:, first : first + CHUNK],
+                    in_=result[:].rearrange("t p e -> t (p e)"),
+                )

import concourse.mybir as mybir
from concourse.masks import make_identity

F32 = mybir.dt.float32
BF16 = mybir.dt.bfloat16
U32 = mybir.dt.uint32
U8 = mybir.dt.uint8
E4M3_X4 = mybir.dt.float8_e4m3fn_x4
E5M2_X4 = mybir.dt.float8_e5m2_x4
MULT = mybir.AluOpType.mult
ADD = mybir.AluOpType.add

P = 128
PACK = 4
T = 128
D = 512
N = 1024
SCALE = N ** -0.5

HALVES = D // 2 // P
PARITIES = 2
CHUNK = P * PARITIES
BANK = 512
N_BANKS = N // BANK
CHUNKS = BANK // CHUNK
TURN_BANKS = 8 - N_BANKS

FLOPS = 2 * T * N * D
BYTES = 2 * (T * D + N * D + 2 * T * N) + 4 * T * N


def transpose_rows(nc, psum, rows, ident):
    words = rows.bitcast(F32)
    turned = psum.tile([P, HALVES, P], F32, tag="turned")
    for u in range(HALVES):
        nc.tensor.transpose(turned[:, u, :], words[:, u * P : (u + 1) * P], ident)
    return turned


def group_words(copy, grouped, turned):
    copy(out=grouped.bitcast(F32), in_=turned[:].rearrange("p u r -> p r u"))


def tile_attention_pb_s_kernel(tc, Q, V, state, cos, sin, grad_out, out):
    nc = tc.nc
    v_dram = V.flatten_outer_dims()
    out_dram = out.flatten_outer_dims()
    g_dram = grad_out.flatten_outer_dims().rearrange("(c p e) d -> c p e d", p=P, e=PARITIES)

    with (
        tc.tile_pool(name="keep", bufs=1) as keep,
        tc.tile_pool(name="banks", bufs=N_BANKS) as banks,
        tc.tile_pool(name="chunks", bufs=N_BANKS * CHUNKS) as chunks,
        tc.tile_pool(name="planes", bufs=N_BANKS * CHUNKS * PARITIES) as planes,
        tc.psum_pool(name="psum_turn", bufs=TURN_BANKS) as psum_turn,
        tc.psum_pool(name="psum_h", bufs=N_BANKS) as psum_h,
        tc.manual_schedule(),
    ):
        ident = keep.tile([P, P], F32)
        make_identity(nc, ident[:])

        v_rows = keep.tile([T, D], BF16)
        nc.sync.dma_start(out=v_rows[:], in_=v_dram)
        g_chunks = []
        for c in range(N_BANKS * CHUNKS):
            g_rows = chunks.tile([P, PARITIES, D], BF16)
            nc.sync.dma_start(out=g_rows[:], in_=g_dram[c])
            g_chunks.append(g_rows)
        sin_banks = []
        cos_banks = []
        for b in range(N_BANKS):
            cols = slice(b * BANK, (b + 1) * BANK)
            sin_sb = banks.tile([T, BANK], BF16)
            nc.sync.dma_start(out=sin_sb[:], in_=sin[:, cols])
            sin_banks.append(sin_sb)
            cos_sb = banks.tile([T, BANK], BF16)
            nc.sync.dma_start(out=cos_sb[:], in_=cos[:, cols])
            cos_banks.append(cos_sb)

        v_grouped = keep.tile([P, T, PACK], BF16, align_bytes=64)
        v_codes = keep.tile([P, T], U32, align_bytes=64)
        v_scales = keep.tile([P, T], U8, align_bytes=64)
        v_turned = transpose_rows(nc, psum_turn, v_rows[:], ident[:])
        group_words(nc.vector.tensor_copy, v_grouped[:], v_turned)
        nc.vector.quantize_mx(
            out=v_codes[:].bitcast(E4M3_X4),
            scales=v_scales[:],
            in_=v_grouped[:].rearrange("p r t -> p (r t)"),
        )

        code_banks = []
        scale_banks = []
        for b in range(N_BANKS):
            g_codes = banks.tile([P, CHUNKS, PARITIES, P], U32, align_bytes=64)
            g_scales = banks.tile([P, CHUNKS, PARITIES, P], U8, align_bytes=64)
            for c in range(CHUNKS):
                for e in range(PARITIES):
                    g_turned = transpose_rows(nc, psum_turn, g_chunks[b * CHUNKS + c][:, e, :], ident[:])
                    g_grouped = planes.tile([P, P, PACK], BF16, align_bytes=64)
                    group_words(nc.scalar.copy, g_grouped[:], g_turned)
                    nc.vector.quantize_mx(
                        out=g_codes[:, c, e, :].bitcast(E5M2_X4),
                        scales=g_scales[:, c, e, :],
                        in_=g_grouped[:].rearrange("p r t -> p (r t)"),
                    )
            code_banks.append(g_codes)
            scale_banks.append(g_scales)

        for b in range(N_BANKS):
            h = psum_h.tile([T, BANK], F32)
            nc.tensor.matmul_mx(
                out=h[:],
                lhsT=v_codes[:].bitcast(E4M3_X4),
                lhsT_scale=v_scales[:],
                rhs=code_banks[b][:].rearrange("p c e r -> p (c e r)").bitcast(E5M2_X4),
                rhs_scale=scale_banks[b][:].rearrange("p c e r -> p (c e r)"),
                start=True,
                stop=True,
            )

            crossed = banks.tile([T, PARITIES, CHUNKS, P], F32)
            h_by_parity = h[:].rearrange("t (c e p) -> t e c p", c=CHUNKS, e=PARITIES)
            sin_by_parity = sin_banks[b][:].rearrange("t (c p e) -> t e c p", c=CHUNKS, e=PARITIES)
            for e in range(PARITIES):
                partner = 1 - e
                nc.vector.scalar_tensor_tensor(
                    out=crossed[:, e, :, :],
                    in0=h_by_parity[:, partner],
                    scalar=SCALE if e == 0 else -SCALE,
                    in1=sin_by_parity[:, partner],
                    op0=MULT,
                    op1=MULT,
                )
            directs = []
            for c in range(CHUNKS):
                cols = slice(c * CHUNK, (c + 1) * CHUNK)
                direct = chunks.tile([T, P, PARITIES], F32)
                nc.vector.scalar_tensor_tensor(
                    out=direct[:],
                    in0=h[:, cols].rearrange("t (e p) -> t p e", e=PARITIES),
                    scalar=SCALE,
                    in1=cos_banks[b][:, cols].rearrange("t (p e) -> t p e", e=PARITIES),
                    op0=MULT,
                    op1=MULT,
                )
                directs.append(direct)
            adder = nc.vector if b == N_BANKS - 1 else nc.gpsimd
            for c in range(CHUNKS):
                result = chunks.tile([T, P, PARITIES], F32)
                adder.tensor_tensor(
                    out=result[:],
                    in0=directs[c][:],
                    in1=crossed[:, :, c, :].rearrange("t e p -> t p e"),
                    op=ADD,
                )
                first = b * BANK + c * CHUNK
                nc.sync.dma_start(
                    out=out_dram[:, first : first + CHUNK],
                    in_=result[:].rearrange("t p e -> t (p e)"),
                )
